import numpy as np
import ml_dtypes


def mxq(x, axis, fmt="e4m3"):
    dtype, down = {"e4m3": (ml_dtypes.float8_e4m3fn, 7), "e5m2": (ml_dtypes.float8_e5m2, 14)}[fmt]
    v = np.moveaxis(np.asarray(x, np.float32).astype(ml_dtypes.bfloat16).astype(np.float64), axis, -1)
    blocks = v.reshape(v.shape[:-1] + (-1, 32))
    amax = np.abs(blocks).max(-1, keepdims=True)
    byte = np.maximum(np.where(amax > 0, np.frexp(amax)[1] - 1 + 127, 0) - down, 1)
    scale = np.exp2(byte - 127.0)
    codes = (blocks / scale).astype(np.float32).astype(dtype).astype(np.float64)
    return np.moveaxis((codes * scale).reshape(v.shape), -1, axis)


WIDE = False


def mx_kscale(k):
    if not WIDE:
        return np.ones(k)
    levels = np.array([10, -10, 5, -5, 0])
    if k % 512:
        return np.exp2(np.random.permutation(np.resize(levels, k // 32))).repeat(32)
    a = np.empty((k // 512, 16))
    for p in range(k // 512):
        a[p, :8] = np.random.permutation(np.resize(levels, 8))
        for g in range(8):
            far = levels[np.abs(levels - a[p, g]) >= 10]
            a[p, g + 8] = far[np.random.randint(len(far))]
    return np.exp2(a.ravel()).repeat(32)


BF16 = ml_dtypes.bfloat16


def bf(x):
    return np.asarray(x, np.float32).astype(BF16)


def f64(x):
    return np.asarray(x).astype(np.float64)


B, A, S, F = 512, 16, 256, 512


def setup_inputs():
    s, u = mx_kscale(F), mx_kscale(F)
    t, v = mx_kscale(F), mx_kscale(F)
    return {
        "h1": bf(np.maximum(np.random.standard_normal((B, A, F)) * 1.4, 0.0) * s),
        "W2": bf(np.random.standard_normal((A, F, F)) * 1.4 / np.sqrt(F) / s[:, None] * t),
        "b2": bf(np.random.standard_normal((A, F)) * 0.2 * t),
        "W3": bf(np.random.standard_normal((A, F, S)) / np.sqrt(F) / t[:, None]),
        "b3": bf(np.random.standard_normal((A, S)) * 0.2),
        "g1": bf(np.maximum(np.random.standard_normal((B, F)) * 1.4, 0.0) * u),
        "V2": bf(np.random.standard_normal((F, F)) * 1.4 / np.sqrt(F) / u[:, None] * v),
        "c2": bf(np.random.standard_normal(F) * 0.2 * v),
        "V3": bf(np.random.standard_normal((F, S)) / np.sqrt(F) / v[:, None]),
        "c3": bf(np.random.standard_normal(S) * 0.2),
    }


def reference(h1, W2, b2, W3, b3, g1, V2, c2, V3, c3):
    ha = mxq(f64(h1), 2, "e4m3").transpose(1, 0, 2)
    h2 = np.maximum((ha @ mxq(f64(W2), 1, "e4m3")) + f64(b2)[:, None, :], 0.0)
    psi_adv = ((mxq(h2, 2, "e4m3") @ mxq(f64(W3), 1, "e4m3")) + f64(b3)[:, None, :]).transpose(1, 0, 2)
    g2 = np.maximum((mxq(f64(g1), 1, "e4m3") @ mxq(f64(V2), 0, "e4m3")) + f64(c2), 0.0)
    psi_state = (mxq(g2, 1, "e4m3") @ mxq(f64(V3), 0, "e4m3")) + f64(c3)
    return psi_state[:, None, :] + psi_adv - psi_adv.mean(axis=1, keepdims=True)

@@ -1,0 +1,427 @@
+from contextlib import ExitStack
+
+import concourse.mybir as mybir
+from concourse.masks import make_identity
+
+FLOPS = 17 * (2 * 512 * 512 * 512 + 2 * 512 * 512 * 256)
+
+F32 = mybir.dt.float32
+BF16 = mybir.dt.bfloat16
+U32 = mybir.dt.uint32
+U8 = mybir.dt.uint8
+FP8X4 = mybir.dt.float8_e4m3fn_x4
+ADD = mybir.AluOpType.add
+MULT = mybir.AluOpType.mult
+RELU = mybir.ActivationFunctionType.Relu
+IDENT = mybir.ActivationFunctionType.Identity
+
+P = 128
+A = 16
+NI = 4
+F = 512
+S = 256
+R3V = 192
+LAST_SUMMED = 14
+NW = A + 1
+RAW_BUFS = 4
+X_BUFS = 3
+
+
+def regroup(engine_copy, dst, src):
+    engine_copy(
+        out=dst.rearrange("p (c i) t -> p c t i", i=4),
+        in_=src.rearrange("p t (c i) -> p c t i", i=4),
+    )
+
+
+def tile_psicritic_pa_kernel(tc, h1, W2, b2, W3, b3, g1, V2, c2, V3, c3, out):
+    nc = tc.nc
+    h1v = h1.rearrange("(i p) a k -> p i a k", p=P)
+    outv = out.rearrange("(i p) a s -> p i a s", p=P)
+
+    with ExitStack() as ctx:
+        const = ctx.enter_context(tc.tile_pool(name="const", bufs=1))
+        xpool = ctx.enter_context(tc.tile_pool(name="xpool", bufs=X_BUFS))
+        rawp = ctx.enter_context(tc.tile_pool(name="rawp", bufs=RAW_BUFS))
+        two = ctx.enter_context(tc.tile_pool(name="two", bufs=2))
+        four = ctx.enter_context(tc.tile_pool(name="four", bufs=4))
+        five = ctx.enter_context(tc.tile_pool(name="five", bufs=5))
+        opool = ctx.enter_context(tc.tile_pool(name="opool", bufs=6))
+        tp_pool = ctx.enter_context(tc.psum_pool(name="tp_pool", bufs=2))
+        l1_pool = ctx.enter_context(tc.psum_pool(name="l1_pool", bufs=2))
+        pp_pool = ctx.enter_context(tc.psum_pool(name="pp_pool", bufs=2))
+        m_pool = ctx.enter_context(tc.psum_pool(name="m_pool", bufs=1))
+        ctx.enter_context(tc.manual_schedule())
+
+        raws = {}
+        xs = {}
+        wg = {}
+        w2q = {}
+        w3q = {}
+        g1s = {}
+        h1q = {}
+        pls = {}
+        g2s = {}
+        h2q = {}
+        pps = {}
+        l1s = {}
+
+        def live(w):
+            return 0 <= w < NW
+
+        def load_w2(w):
+            w2raw = rawp.tile([P, 4, F], BF16, name="w2raw")
+            nc.sync.dma_start(
+                out=w2raw[:], in_=(V2 if w == 0 else W2[w - 1]).rearrange("(p j) n -> p j n", j=4)
+            )
+            raws[(2, w)] = w2raw
+
+        def load_w3(w):
+            w3raw = rawp.tile([P, 4, S], BF16, name="w3raw")
+            nc.sync.dma_start(
+                out=w3raw[:], in_=(V3 if w == 0 else W3[w - 1]).rearrange("(p j) s -> p j s", j=4)
+            )
+            raws[(3, w)] = w3raw
+
+        def load_x(pair):
+            xt = xpool.tile([P, NI, 2, F], BF16, name="xt")
+            nc.sync.dma_start(out=xt[:], in_=h1v[:, :, 2 * pair : 2 * pair + 2, :])
+            xs[pair] = xt
+
+        def load_x_half(pair, al):
+            nc.sync.dma_start(out=xs[pair][:, :, al, :], in_=h1v[:, :, 2 * pair + al, :])
+
+        ident = const.tile([P, P], F32, name="ident")
+        make_identity(nc, ident[:])
+        brow = const.tile([P, F], BF16, name="brow")
+        nc.vector.memset(brow[:], 0.0)
+        nc.scalar.dma_start(out=brow[0:1, :], in_=c2.rearrange("(o f) -> o f", o=1))
+        nc.scalar.dma_start(out=brow[1:17, :], in_=b2)
+        b3rows = const.tile([P, S], BF16, name="b3rows")
+        nc.vector.memset(b3rows[:], 0.0)
+        nc.scalar.dma_start(out=b3rows[0:16, :], in_=b3)
+        nc.scalar.dma_start(out=b3rows[16:17, :], in_=c3.rearrange("(o s) -> o s", o=1))
+        lmean = const.tile([P, P], BF16, name="lmean")
+        nc.vector.memset(lmean[:], 0.0)
+        nc.vector.memset(lmean[0:17, :], 1.0)
+        nc.vector.memset(lmean[0:16, :], -1.0 / A)
+
+        xg = const.tile([P, NI, F], BF16, name="xg")
+        load_w2(0)
+        nc.sync.dma_start(out=xg[:], in_=g1.rearrange("(i p) k -> p i k", p=P))
+        load_w3(0)
+        xs[0] = xpool.tile([P, NI, 2, F], BF16, name="xt")
+        load_x_half(0, 0)
+        load_w2(1)
+        load_w3(1)
+        load_x_half(0, 1)
+        load_w2(2)
+        load_w3(2)
+        load_x(1)
+        load_w2(3)
+        load_w3(3)
+        load_x(2)
+
+        browf = const.tile([P, 4, P], F32, name="browf")
+        nc.vector.tensor_copy(out=browf[:], in_=brow[:].rearrange("p (m t) -> p t m", t=4))
+        b3f = const.tile([P, 2, P], F32, name="b3f")
+        nc.vector.tensor_copy(out=b3f[:], in_=b3rows[:].rearrange("p (t m) -> p t m", t=2))
+        tpb = pp_pool.tile([P, 2, S], F32, name="tpb", tag="pp")
+        for t in range(4):
+            nc.tensor.transpose(tpb[:, t // 2, P * (t % 2) : P * (t % 2) + P], browf[:, t, :], ident[:])
+        bias2 = const.tile([P, 4, NW], F32, name="bias2")
+        for u in range(2):
+            nc.vector.tensor_copy(
+                out=bias2[:, 2 * u : 2 * u + 2, :],
+                in_=tpb[:, u, :].rearrange("p (t w) -> p t w", t=2)[:, :, 0:NW],
+            )
+        tpb3 = pp_pool.tile([P, 2, S], F32, name="tpb3", tag="pp")
+        for t in range(2):
+            nc.tensor.transpose(tpb3[:, 0, P * t : P * t + P], b3f[:, t, :], ident[:])
+        bias3 = const.tile([P, 2, A], F32, name="bias3")
+        nc.vector.tensor_copy(
+            out=bias3[:], in_=tpb3[:, 0, :].rearrange("p (t a) -> p t a", t=2)[:, :, 0:A]
+        )
+        tpg = pp_pool.tile([P, 2, S], F32, name="tpg", tag="pp")
+        nc.tensor.matmul(tpg[:, 0, :], lhsT=lmean[:], rhs=b3rows[:], start=True, stop=True)
+        gam = const.tile([P, S], F32, name="gam")
+        nc.vector.tensor_copy(out=gam[:], in_=tpg[:, 0, :])
+
+        advt = const.tile([P, A, 2, F], F32, name="advt")
+        sg = const.tile([P, NI, S], F32, name="sg")
+        dpre = const.tile([P, NI, S], F32, name="dpre")
+        dfin = const.tile([P, NI, S], F32, name="dfin")
+        mts = const.tile([P, 2, F], F32, name="mts")
+        mt = [m_pool.tile([P, F], F32, name="mt%d" % st) for st in range(2)]
+
+        def mx(dst, lc, ls, lcols, rc, rs, start, stop):
+            nc.tensor.matmul_mx(
+                out=dst,
+                lhsT=lc[:, lcols].bitcast(FP8X4),
+                lhsT_scale=ls[:, lcols],
+                rhs=rc[:].bitcast(FP8X4),
+                rhs_scale=rs[:],
+                start=start,
+                stop=stop,
+            )
+
+        def quantise(pool, width, src, cname, sname):
+            codes = pool.tile([P, width], U32, name=cname, align_bytes=64)
+            scales = pool.tile([P, width], U8, name=sname, align_bytes=64)
+            nc.vector.quantize_mx(
+                out=codes[:].bitcast(FP8X4), scales=scales[:], in_=src[:].rearrange("p n t -> p (n t)")
+            )
+            return codes, scales
+
+        def regroup_weights(w):
+            w2g = two.tile([P, F, 4], BF16, name="w2g", align_bytes=64)
+            nc.vector.tensor_copy(
+                out=w2g[:].rearrange("p (t m) j -> p m j t", t=4),
+                in_=raws[(2, w)][:].rearrange("p j (m t) -> p m j t", t=4),
+            )
+            w3g = two.tile([P, S, 4], BF16, name="w3g", align_bytes=64)
+            regroup(nc.vector.tensor_copy, w3g[:, 0:R3V, :], raws[(3, w)][:, :, 0:R3V])
+            regroup(nc.scalar.copy, w3g[:, R3V:S, :], raws[(3, w)][:, :, R3V:S])
+            wg[w] = (w2g, w3g)
+
+        def transpose_x(w):
+            if w == 0:
+                xw = xg[:].bitcast(F32)
+            else:
+                xw = xs[(w - 1) // 2][:].bitcast(F32)[:, :, (w - 1) % 2, :]
+            g1t = two.tile([P, F, 4], BF16, name="g1t", align_bytes=64)
+            g1w = g1t[:].bitcast(F32)
+            for ih in range(2):
+                tp = tp_pool.tile([P, 2, S], F32, name="tp", tag="tp")
+                for il in range(2):
+                    for u in range(2):
+                        nc.tensor.transpose(
+                            tp[:, u, P * il : P * il + P],
+                            xw[:, 2 * ih + il, u::2],
+                            ident[:],
+                        )
+                nc.scalar.copy(
+                    out=g1w[:, S * ih : S * ih + S, :], in_=tp[:].rearrange("p u b -> p b u")
+                )
+            g1s[w] = g1t
+
+        def layer1(w, t, pool, tag):
+            w2c, w2s = w2q[w]
+            h1c, h1s = h1q[w]
+            l1 = pool.tile([P, F], F32, name="l1", tag=tag)
+            mx(l1[:], w2c, w2s, slice(P * t, P * t + P), h1c, h1s, True, True)
+            l1s[(w, t)] = l1
+
+        def relu_out(w, t, cols, dst):
+            nc.scalar.activation(
+                out=dst[:, t, :],
+                in_=l1s[(w, t)][:, cols],
+                func=RELU,
+                bias=bias2[:, t, w : w + 1],
+                scale=1.0,
+            )
+
+        def layer1_step(w):
+            pls[w] = two.tile([P, 4, F], BF16, name="planes")
+            for t in range(4):
+                layer1(w, t, l1_pool, "l1")
+                relu_out(w, t, slice(0, F), pls[w])
+                if 1 <= t <= 2 and live(w - 2):
+                    leave_psum(w - 2, t - 1)
+
+        def regroup_hidden(w):
+            g2t = two.tile([P, F, 4], BF16, name="g2t", align_bytes=64)
+            regroup(nc.vector.tensor_copy, g2t[:], pls[w][:])
+            g2s[w] = g2t
+
+        def batch_major(w, pool, tag):
+            w3c, w3s = w3q[w]
+            h2c, h2s = h2q[w]
+            for ih in range(2):
+                pq = pool.tile([P, 2, S], F32, name="pq", tag=tag)
+                for il in range(2):
+                    i = 2 * ih + il
+                    mx(pq[:, il, :], h2c, h2s, slice(P * i, P * i + P), w3c, w3s, True, True)
+                pps[(w, ih)] = pq
+
+        def feature_major(w, st, pool, tag):
+            w3c, w3s = w3q[w]
+            h2c, h2s = h2q[w]
+            pt = pool.tile([P, F], F32, name="pt", tag=tag)
+            mx(pt[:], w3c, w3s, slice(P * st, P * st + P), h2c, h2s, True, True)
+            pps[(-w, st)] = pt
+
+        def add_to_sum(w, st):
+            w3c, w3s = w3q[w]
+            h2c, h2s = h2q[w]
+            mx(mt[st][:], w3c, w3s, slice(P * st, P * st + P), h2c, h2s, w == 1, w == LAST_SUMMED)
+
+        def layer2(w):
+            if w == 0:
+                batch_major(w, pp_pool, "pp")
+                return
+            for st in range(2):
+                feature_major(w, st, pp_pool, "pp")
+                add_to_sum(w, st)
+
+        def leave_psum(w, half):
+            if w == 0:
+                pair = slice(2 * half, 2 * half + 2)
+                nc.vector.tensor_tensor(
+                    out=sg[:, pair, :],
+                    in0=pps[(w, half)][:],
+                    in1=gam[:].unsqueeze(1).to_broadcast([P, 2, S]),
+                    op=ADD,
+                )
+                return
+            nc.scalar.activation(
+                out=advt[:, w - 1, half, :],
+                in_=pps[(-w, half)][:],
+                func=IDENT,
+                bias=bias3[:, half, w - 1 : w],
+                scale=1.0,
+            )
+
+        for n in range(-2, LAST_SUMMED + 1):
+            if live(n - 1):
+                regroup_hidden(n - 1)
+            if live(n):
+                layer1_step(n)
+            if live(n + 1):
+                w2q[n + 1] = quantise(two, F, wg[n + 1][0], "w2c", "w2s")
+                h1q[n + 1] = quantise(two, F, g1s[n + 1], "h1c", "h1s")
+            if live(n - 1):
+                h2q[n - 1] = quantise(four, F, g2s[n - 1], "h2c", "h2s")
+            if live(n + 2):
+                transpose_x(n + 2)
+            if live(n - 1):
+                layer2(n - 1)
+            if live(n + 2):
+                regroup_weights(n + 2)
+            if live(n + 1):
+                w3q[n + 1] = quantise(five, S, wg[n + 1][1], "w3c", "w3s")
+            if live(n + 2 + RAW_BUFS):
+                load_w2(n + 2 + RAW_BUFS)
+                load_w3(n + 2 + RAW_BUFS)
+            if n >= 0 and n % 2 == 0 and n // 2 + X_BUFS < A // 2:
+                load_x(n // 2 + X_BUFS)
+
+        w_a, w_b, w_c = LAST_SUMMED, LAST_SUMMED + 1, LAST_SUMMED + 2
+        regroup_hidden(w_a)
+        layer1_step(w_b)
+        w2q[w_c] = quantise(two, F, wg[w_c][0], "w2c", "w2s")
+        h1q[w_c] = quantise(two, F, g1s[w_c], "h1c", "h1s")
+        layer1(w_c, 0, tp_pool, "tp")
+        layer1(w_c, 1, tp_pool, "tp")
+        h2q[w_a] = quantise(four, F, g2s[w_a], "h2c", "h2s")
+        add_to_sum(w_a, 0)
+        add_to_sum(w_a, 1)
+        layer1(w_c, 2, l1_pool, "l1")
+        layer1(w_c, 3, l1_pool, "l1")
+        w3q[w_c] = quantise(five, S, wg[w_c][1], "w3c", "w3s")
+
+        halves = [slice(0, S), slice(S, F)]
+        plh = [None, None]
+        g2h = [None, None]
+        plh[0] = two.tile([P, 4, S], BF16, name="planes")
+        for t in range(4):
+            relu_out(w_c, t, halves[0], plh[0])
+        for st in range(2):
+            nc.scalar.copy(out=mts[:, st, :], in_=mt[st][:])
+        regroup_hidden(w_b)
+        plh[1] = two.tile([P, 4, S], BF16, name="planes")
+        for t in range(4):
+            relu_out(w_c, t, halves[1], plh[1])
+
+        h2c_c = four.tile([P, F], U32, name="h2c", align_bytes=64)
+        h2s_c = four.tile([P, F], U8, name="h2s", align_bytes=64)
+        h2q[w_c] = (h2c_c, h2s_c)
+
+        def regroup_last(h):
+            g2h[h] = two.tile([P, S, 4], BF16, name="g2t", align_bytes=64)
+            regroup(nc.vector.tensor_copy, g2h[h][:], plh[h][:])
+
+        def quantise_last(h):
+            nc.vector.quantize_mx(
+                out=h2c_c[:, halves[h]].bitcast(FP8X4),
+                scales=h2s_c[:, halves[h]],
+                in_=g2h[h][:].rearrange("p n t -> p (n t)"),
+            )
+
+        mbs = [None, None]
+        pqs = [None, None]
+
+        def turn_sum(ih):
+            mbs[ih] = m_pool.tile([P, 2, S], F32, name="mb", tag="mt%d" % ih)
+            for il in range(2):
+                for st in range(2):
+                    nc.tensor.transpose(
+                        mbs[ih][:, il, P * st : P * st + P],
+                        mts[:, st, P * (2 * ih + il) : P * (2 * ih + il) + P],
+                        ident[:],
+                    )
+
+        def last_two_products(ih):
+            pqs[ih] = pp_pool.tile([P, 2, S], F32, name="pq", tag="pp")
+            for il in range(2):
+                cols = slice(P * (2 * ih + il), P * (2 * ih + il) + P)
+                for w in (w_b, w_c):
+                    mx(pqs[ih][:, il, :], h2q[w][0], h2q[w][1], cols, w3q[w][0], w3q[w][1], w == w_b, w == w_c)
+
+        def minus_mean(dst, src, base, ih):
+            pair = slice(2 * ih, 2 * ih + 2)
+            nc.vector.scalar_tensor_tensor(
+                out=dst[:, pair, :], in0=src[:], scalar=-1.0 / A, in1=base[:, pair, :], op0=MULT, op1=ADD
+            )
+
+        def late_product(w):
+            for st in range(2):
+                feature_major(w, st, m_pool, "mt%d" % st)
+                leave_psum(w, st)
+
+        regroup_last(0)
+        h2q[w_b] = quantise(four, F, g2s[w_b], "h2c", "h2s")
+        quantise_last(0)
+        turn_sum(0)
+        last_two_products(0)
+        minus_mean(dpre, mbs[0], sg, 0)
+        minus_mean(dfin, pqs[0], dpre, 0)
+
+        chunks = (
+            [(i, c) for i in (0, 1) for c in range(3)]
+            + [(i, c) for i in (2, 3) for c in range(3)]
+            + [(i, 3) for i in range(NI)]
+        )
+        banks = [(l1_pool, "l1"), (tp_pool, "tp")]
+        for k, (i, c) in enumerate(chunks):
+            ost = opool.tile([P, 4, S], F32, name="ost")
+            for h in range(2):
+                pool, tag = banks[h]
+                fin = pool.tile([P, 2, S], F32, name="fin", tag=tag)
+                for al in range(2):
+                    for st in range(2):
+                        nc.tensor.transpose(
+                            fin[:, al, P * st : P * st + P],
+                            advt[:, 4 * c + 2 * h + al, st, P * i : P * i + P],
+                            ident[:],
+                        )
+                nc.vector.tensor_tensor(
+                    out=ost[:, 2 * h : 2 * h + 2, :],
+                    in0=fin[:],
+                    in1=dfin[:, i, :].unsqueeze(1).to_broadcast([P, 2, S]),
+                    op=ADD,
+                )
+            nc.sync.dma_start(out=outv[:, i, 4 * c : 4 * c + 4, :], in_=ost[:])
+            if k == 0:
+                regroup_last(1)
+            if k == 1:
+                turn_sum(1)
+                quantise_last(1)
+            if k == 2:
+                minus_mean(dpre, mbs[1], sg, 1)
+            if k == 3:
+                last_two_products(1)
+            if k == 4:
+                minus_mean(dfin, pqs[1], dpre, 1)
+            if k in (5, 7, 9):
+                late_product(w_a + (k - 5) // 2)

@@ -12,6 +12,7 @@ U8 = mybir.dt.uint8
 FP8X4 = mybir.dt.float8_e4m3fn_x4
 ADD = mybir.AluOpType.add
 MULT = mybir.AluOpType.mult
+AXIS_X = mybir.AxisListType.X
 RELU = mybir.ActivationFunctionType.Relu
 IDENT = mybir.ActivationFunctionType.Identity
 
@@ -20,18 +21,15 @@ A = 16
 NI = 4
 F = 512
 S = 256
-R3V = 192
-LAST_SUMMED = 14
+R3V = 40
 NW = A + 1
+DIRECT = (4, 6, 8, 10, 12, 14, 16)
 RAW_BUFS = 4
 X_BUFS = 3
 
 
-def regroup(engine_copy, dst, src):
-    engine_copy(
-        out=dst.rearrange("p (c i) t -> p c t i", i=4),
-        in_=src.rearrange("p t (c i) -> p c t i", i=4),
-    )
+def grouped(dst, src):
+    return dst.rearrange("p (c i) t -> p c t i", i=4), src.rearrange("p t (c i) -> p c t i", i=4)
 
 
 def tile_psicritic_pa_kernel(tc, h1, W2, b2, W3, b3, g1, V2, c2, V3, c3, out):
@@ -44,27 +42,29 @@ def tile_psicritic_pa_kernel(tc, h1, W2, b2, W3, b3, g1, V2, c2, V3, c3, out):
         xpool = ctx.enter_context(tc.tile_pool(name="xpool", bufs=X_BUFS))
         rawp = ctx.enter_context(tc.tile_pool(name="rawp", bufs=RAW_BUFS))
         two = ctx.enter_context(tc.tile_pool(name="two", bufs=2))
-        four = ctx.enter_context(tc.tile_pool(name="four", bufs=4))
-        five = ctx.enter_context(tc.tile_pool(name="five", bufs=5))
-        opool = ctx.enter_context(tc.tile_pool(name="opool", bufs=6))
+        opool = ctx.enter_context(tc.tile_pool(name="opool", bufs=5))
+        nstp = ctx.enter_context(tc.tile_pool(name="nstp", bufs=3))
+        dap = ctx.enter_context(tc.tile_pool(name="dap", bufs=3))
         tp_pool = ctx.enter_context(tc.psum_pool(name="tp_pool", bufs=2))
-        l1_pool = ctx.enter_context(tc.psum_pool(name="l1_pool", bufs=2))
-        pp_pool = ctx.enter_context(tc.psum_pool(name="pp_pool", bufs=2))
+        l1_pool = ctx.enter_context(tc.psum_pool(name="l1_pool", bufs=4))
         m_pool = ctx.enter_context(tc.psum_pool(name="m_pool", bufs=1))
         ctx.enter_context(tc.manual_schedule())
 
         raws = {}
         xs = {}
-        wg = {}
+        firsts = {}
+        wg3 = {}
         w2q = {}
         w3q = {}
-        g1s = {}
         h1q = {}
         pls = {}
         g2s = {}
         h2q = {}
         pps = {}
         l1s = {}
+        nsts = {}
+        das = {}
+        osts = {}
 
         def live(w):
             return 0 <= w < NW
@@ -95,63 +95,60 @@ def tile_psicritic_pa_kernel(tc, h1, W2, b2, W3, b3, g1, V2, c2, V3, c3, out):
         make_identity(nc, ident[:])
         brow = const.tile([P, F], BF16, name="brow")
         nc.vector.memset(brow[:], 0.0)
-        nc.scalar.dma_start(out=brow[0:1, :], in_=c2.rearrange("(o f) -> o f", o=1))
-        nc.scalar.dma_start(out=brow[1:17, :], in_=b2)
         b3rows = const.tile([P, S], BF16, name="b3rows")
         nc.vector.memset(b3rows[:], 0.0)
-        nc.scalar.dma_start(out=b3rows[0:16, :], in_=b3)
-        nc.scalar.dma_start(out=b3rows[16:17, :], in_=c3.rearrange("(o s) -> o s", o=1))
-        lmean = const.tile([P, P], BF16, name="lmean")
-        nc.vector.memset(lmean[:], 0.0)
-        nc.vector.memset(lmean[0:17, :], 1.0)
-        nc.vector.memset(lmean[0:16, :], -1.0 / A)
 
         xg = const.tile([P, NI, F], BF16, name="xg")
         load_w2(0)
         nc.sync.dma_start(out=xg[:], in_=g1.rearrange("(i p) k -> p i k", p=P))
-        load_w3(0)
+        load_w2(1)
+        nc.sync.dma_start(out=brow[1:NW, :], in_=b2)
+        nc.sync.dma_start(out=brow[0:1, :], in_=c2.rearrange("(o f) -> o f", o=1))
         xs[0] = xpool.tile([P, NI, 2, F], BF16, name="xt")
         load_x_half(0, 0)
-        load_w2(1)
-        load_w3(1)
-        load_x_half(0, 1)
         load_w2(2)
-        load_w3(2)
-        load_x(1)
+        nc.sync.dma_start(out=b3rows[0:A, :], in_=b3)
+        nc.sync.dma_start(out=b3rows[A:NW, :], in_=c3.rearrange("(o s) -> o s", o=1))
+        load_w3(0)
+        load_x_half(0, 1)
+        load_w3(1)
         load_w2(3)
+        load_x(1)
+        load_w3(2)
         load_w3(3)
         load_x(2)
 
-        browf = const.tile([P, 4, P], F32, name="browf")
-        nc.vector.tensor_copy(out=browf[:], in_=brow[:].rearrange("p (m t) -> p t m", t=4))
-        b3f = const.tile([P, 2, P], F32, name="b3f")
-        nc.vector.tensor_copy(out=b3f[:], in_=b3rows[:].rearrange("p (t m) -> p t m", t=2))
-        tpb = pp_pool.tile([P, 2, S], F32, name="tpb", tag="pp")
-        for t in range(4):
-            nc.tensor.transpose(tpb[:, t // 2, P * (t % 2) : P * (t % 2) + P], browf[:, t, :], ident[:])
         bias2 = const.tile([P, 4, NW], F32, name="bias2")
-        for u in range(2):
-            nc.vector.tensor_copy(
-                out=bias2[:, 2 * u : 2 * u + 2, :],
-                in_=tpb[:, u, :].rearrange("p (t w) -> p t w", t=2)[:, :, 0:NW],
-            )
-        tpb3 = pp_pool.tile([P, 2, S], F32, name="tpb3", tag="pp")
-        for t in range(2):
-            nc.tensor.transpose(tpb3[:, 0, P * t : P * t + P], b3f[:, t, :], ident[:])
-        bias3 = const.tile([P, 2, A], F32, name="bias3")
-        nc.vector.tensor_copy(
-            out=bias3[:], in_=tpb3[:, 0, :].rearrange("p (t a) -> p t a", t=2)[:, :, 0:A]
-        )
-        tpg = pp_pool.tile([P, 2, S], F32, name="tpg", tag="pp")
-        nc.tensor.matmul(tpg[:, 0, :], lhsT=lmean[:], rhs=b3rows[:], start=True, stop=True)
-        gam = const.tile([P, S], F32, name="gam")
-        nc.vector.tensor_copy(out=gam[:], in_=tpg[:, 0, :])
+        bias3 = const.tile([P, 2, NW], F32, name="bias3")
+        gamt = const.tile([P, 2, 1], F32, name="gamt")
+        b3all = const.tile([P, A // 2, S], BF16, name="b3all")
 
-        advt = const.tile([P, A, 2, F], F32, name="advt")
-        sg = const.tile([P, NI, S], F32, name="sg")
-        dpre = const.tile([P, NI, S], F32, name="dpre")
+        def prepare_b2():
+            browf = const.tile([P, 4, P], F32, name="browf")
+            nc.vector.tensor_copy(out=browf[:], in_=brow[:].rearrange("p (m t) -> p t m", t=4))
+            tpb = l1_pool.tile([P, 4, P], F32, name="tpb", tag="l1")
+            for t in range(4):
+                nc.tensor.transpose(tpb[:, t, :], browf[:, t, :], ident[:])
+            nc.scalar.copy(out=bias2[:], in_=tpb[:, :, 0:NW])
+
+        def prepare_b3():
+            b3f = const.tile([P, 2, P], F32, name="b3f")
+            nc.vector.tensor_copy(out=b3f[:], in_=b3rows[:].rearrange("p (t m) -> p t m", t=2))
+            tpb3 = tp_pool.tile([P, 2, P], F32, name="tpb3", tag="tp")
+            for st in range(2):
+                nc.tensor.transpose(tpb3[:, st, :], b3f[:, st, :], ident[:])
+            nc.scalar.copy(out=bias3[:], in_=tpb3[:, :, 0:NW])
+
+        def prepare_gamma():
+            bsum = const.tile([P, 2, 1], F32, name="bsum")
+            for st in range(2):
+                nc.vector.tensor_reduce(out=bsum[:, st, :], in_=bias3[:, st, 0:A], axis=AXIS_X, op=ADD)
+            nc.vector.scalar_tensor_tensor(
+                out=gamt[:], in0=bsum[:], scalar=-1.0 / A, in1=bias3[:, :, A:NW], op0=MULT, op1=ADD
+            )
+
+        dt = const.tile([P, 2, F], F32, name="dt")
         dfin = const.tile([P, NI, S], F32, name="dfin")
-        mts = const.tile([P, 2, F], F32, name="mts")
         mt = [m_pool.tile([P, F], F32, name="mt%d" % st) for st in range(2)]
 
         def mx(dst, lc, ls, lcols, rc, rs, start, stop):
@@ -173,255 +170,235 @@ def tile_psicritic_pa_kernel(tc, h1, W2, b2, W3, b3, g1, V2, c2, V3, c3, out):
             )
             return codes, scales
 
-        def regroup_weights(w):
-            w2g = two.tile([P, F, 4], BF16, name="w2g", align_bytes=64)
+        def quantise_first(w):
+            codes, scales = quantise(two, 2 * F, firsts[w], "fc", "fs")
+            w2q[w] = (codes[:, 0:F], scales[:, 0:F])
+            h1q[w] = (codes[:, F : 2 * F], scales[:, F : 2 * F])
+
+        def first_tile(w):
+            if w not in firsts:
+                firsts[w] = two.tile([P, 2 * F, 4], BF16, name="first", align_bytes=64)
+            return firsts[w]
+
+        def quantise_hidden(w):
+            h2q[w] = quantise(const, F, g2s[w], "h2c%d" % w, "h2s%d" % w)
+
+        def quantise_w3(w):
+            w3q[w] = quantise(const, S, wg3[w], "w3c%d" % w, "w3s%d" % w)
+
+        def regroup_w2(w):
             nc.vector.tensor_copy(
-                out=w2g[:].rearrange("p (t m) j -> p m j t", t=4),
+                out=first_tile(w)[:, 0:F, :].rearrange("p (t m) j -> p m j t", t=4),
                 in_=raws[(2, w)][:].rearrange("p j (m t) -> p m j t", t=4),
             )
+
+        def regroup_w3(w):
             w3g = two.tile([P, S, 4], BF16, name="w3g", align_bytes=64)
-            regroup(nc.vector.tensor_copy, w3g[:, 0:R3V, :], raws[(3, w)][:, :, 0:R3V])
-            regroup(nc.scalar.copy, w3g[:, R3V:S, :], raws[(3, w)][:, :, R3V:S])
-            wg[w] = (w2g, w3g)
+            raw = raws[(3, w)]
+            dst, src = grouped(w3g[:, R3V:S, :], raw[:, :, R3V:S])
+            if w == 0:
+                nc.scalar.mul(dst, src, -float(A))
+            else:
+                nc.scalar.copy(out=dst, in_=src)
+            dst, src = grouped(w3g[:, 0:R3V, :], raw[:, :, 0:R3V])
+            if w == 0:
+                nc.vector.tensor_scalar_mul(dst, src, -float(A))
+            else:
+                nc.vector.tensor_copy(out=dst, in_=src)
+            wg3[w] = w3g
 
         def transpose_x(w):
             if w == 0:
                 xw = xg[:].bitcast(F32)
             else:
                 xw = xs[(w - 1) // 2][:].bitcast(F32)[:, :, (w - 1) % 2, :]
-            g1t = two.tile([P, F, 4], BF16, name="g1t", align_bytes=64)
-            g1w = g1t[:].bitcast(F32)
+            g1w = first_tile(w)[:, F : 2 * F, :].bitcast(F32)
             for ih in range(2):
                 tp = tp_pool.tile([P, 2, S], F32, name="tp", tag="tp")
                 for il in range(2):
                     for u in range(2):
                         nc.tensor.transpose(
-                            tp[:, u, P * il : P * il + P],
-                            xw[:, 2 * ih + il, u::2],
-                            ident[:],
+                            tp[:, u, P * il : P * il + P], xw[:, 2 * ih + il, u::2], ident[:]
                         )
                 nc.scalar.copy(
                     out=g1w[:, S * ih : S * ih + S, :], in_=tp[:].rearrange("p u b -> p b u")
                 )
-            g1s[w] = g1t
 
-        def layer1(w, t, pool, tag):
+        def layer1(w):
             w2c, w2s = w2q[w]
             h1c, h1s = h1q[w]
-            l1 = pool.tile([P, F], F32, name="l1", tag=tag)
-            mx(l1[:], w2c, w2s, slice(P * t, P * t + P), h1c, h1s, True, True)
-            l1s[(w, t)] = l1
+            for t in range(4):
+                l1 = l1_pool.tile([P, F], F32, name="l1", tag="l1")
+                mx(l1[:], w2c, w2s, slice(P * t, P * t + P), h1c, h1s, True, True)
+                l1s[(w, t)] = l1
 
-        def relu_out(w, t, cols, dst):
-            nc.scalar.activation(
-                out=dst[:, t, :],
-                in_=l1s[(w, t)][:, cols],
-                func=RELU,
-                bias=bias2[:, t, w : w + 1],
-                scale=1.0,
-            )
-
-        def layer1_step(w):
+        def relu_out(w):
             pls[w] = two.tile([P, 4, F], BF16, name="planes")
             for t in range(4):
-                layer1(w, t, l1_pool, "l1")
-                relu_out(w, t, slice(0, F), pls[w])
-                if 1 <= t <= 2 and live(w - 2):
-                    leave_psum(w - 2, t - 1)
+                nc.scalar.activation(
+                    out=pls[w][:, t, :],
+                    in_=l1s[(w, t)][:],
+                    func=RELU,
+                    bias=bias2[:, t, w : w + 1],
+                    scale=1.0,
+                )
 
         def regroup_hidden(w):
             g2t = two.tile([P, F, 4], BF16, name="g2t", align_bytes=64)
-            regroup(nc.vector.tensor_copy, g2t[:], pls[w][:])
+            dst, src = grouped(g2t[:], pls[w][:])
+            nc.vector.tensor_copy(out=dst, in_=src)
             g2s[w] = g2t
 
-        def batch_major(w, pool, tag):
-            w3c, w3s = w3q[w]
-            h2c, h2s = h2q[w]
-            for ih in range(2):
-                pq = pool.tile([P, 2, S], F32, name="pq", tag=tag)
-                for il in range(2):
-                    i = 2 * ih + il
-                    mx(pq[:, il, :], h2c, h2s, slice(P * i, P * i + P), w3c, w3s, True, True)
-                pps[(w, ih)] = pq
+        def layer2(w, st, dst, start, stop):
+            mx(dst, w3q[w][0], w3q[w][1], slice(P * st, P * st + P), h2q[w][0], h2q[w][1], start, stop)
 
-        def feature_major(w, st, pool, tag):
-            w3c, w3s = w3q[w]
-            h2c, h2s = h2q[w]
-            pt = pool.tile([P, F], F32, name="pt", tag=tag)
-            mx(pt[:], w3c, w3s, slice(P * st, P * st + P), h2c, h2s, True, True)
-            pps[(-w, st)] = pt
-
-        def add_to_sum(w, st):
-            w3c, w3s = w3q[w]
-            h2c, h2s = h2q[w]
-            mx(mt[st][:], w3c, w3s, slice(P * st, P * st + P), h2c, h2s, w == 1, w == LAST_SUMMED)
-
-        def layer2(w):
-            if w == 0:
-                batch_major(w, pp_pool, "pp")
-                return
+        def add_to_sum(w):
             for st in range(2):
-                feature_major(w, st, pp_pool, "pp")
-                add_to_sum(w, st)
+                layer2(w, st, mt[st][:], w == 0, w == A)
 
-        def leave_psum(w, half):
-            if w == 0:
-                pair = slice(2 * half, 2 * half + 2)
-                nc.vector.tensor_tensor(
-                    out=sg[:, pair, :],
-                    in0=pps[(w, half)][:],
-                    in1=gam[:].unsqueeze(1).to_broadcast([P, 2, S]),
-                    op=ADD,
-                )
-                return
-            nc.scalar.activation(
-                out=advt[:, w - 1, half, :],
-                in_=pps[(-w, half)][:],
-                func=IDENT,
-                bias=bias3[:, half, w - 1 : w],
-                scale=1.0,
-            )
-
-        for n in range(-2, LAST_SUMMED + 1):
+        def step(n):
             if live(n - 1):
                 regroup_hidden(n - 1)
             if live(n):
-                layer1_step(n)
+                relu_out(n)
+                regroup_w3(n)
             if live(n + 1):
-                w2q[n + 1] = quantise(two, F, wg[n + 1][0], "w2c", "w2s")
-                h1q[n + 1] = quantise(two, F, g1s[n + 1], "h1c", "h1s")
+                if n < 1:
+                    regroup_w2(n + 2)
+                quantise_first(n + 1)
             if live(n - 1):
-                h2q[n - 1] = quantise(four, F, g2s[n - 1], "h2c", "h2s")
+                quantise_hidden(n - 1)
             if live(n + 2):
                 transpose_x(n + 2)
-            if live(n - 1):
-                layer2(n - 1)
-            if live(n + 2):
-                regroup_weights(n + 2)
+            if n == -1:
+                prepare_b2()
             if live(n + 1):
-                w3q[n + 1] = quantise(five, S, wg[n + 1][1], "w3c", "w3s")
+                layer1(n + 1)
+            if live(n - 1):
+                quantise_w3(n - 1)
+                add_to_sum(n - 1)
+            if live(n + 2) and (n < -1 or n > 0):
+                regroup_w2(n + 2)
+            if n == 2:
+                prepare_b3()
+            if n == 3:
+                prepare_gamma()
             if live(n + 2 + RAW_BUFS):
                 load_w2(n + 2 + RAW_BUFS)
-                load_w3(n + 2 + RAW_BUFS)
+            if live(n + RAW_BUFS) and n >= 0:
+                load_w3(n + RAW_BUFS)
             if n >= 0 and n % 2 == 0 and n // 2 + X_BUFS < A // 2:
                 load_x(n // 2 + X_BUFS)
+            if n == A // 2:
+                nc.sync.dma_start(
+                    out=b3all[:],
+                    in_=b3.rearrange("(k two) s -> two k s", two=2)[1, :, :].partition_broadcast(P),
+                )
 
-        w_a, w_b, w_c = LAST_SUMMED, LAST_SUMMED + 1, LAST_SUMMED + 2
-        regroup_hidden(w_a)
-        layer1_step(w_b)
-        w2q[w_c] = quantise(two, F, wg[w_c][0], "w2c", "w2s")
-        h1q[w_c] = quantise(two, F, g1s[w_c], "h1c", "h1s")
-        layer1(w_c, 0, tp_pool, "tp")
-        layer1(w_c, 1, tp_pool, "tp")
-        h2q[w_a] = quantise(four, F, g2s[w_a], "h2c", "h2s")
-        add_to_sum(w_a, 0)
-        add_to_sum(w_a, 1)
-        layer1(w_c, 2, l1_pool, "l1")
-        layer1(w_c, 3, l1_pool, "l1")
-        w3q[w_c] = quantise(five, S, wg[w_c][1], "w3c", "w3s")
+        def products(w):
+            if w in DIRECT:
+                for ih in range(2):
+                    pt = l1_pool.tile([P, 2, S], F32, name="pt", tag="l1")
+                    for il in range(2):
+                        i = 2 * ih + il
+                        mx(pt[:, il, :], h2q[w][0], h2q[w][1], slice(P * i, P * i + P), w3q[w][0], w3q[w][1], True, True)
+                    pps[(w, ih)] = pt
+                return
+            for st in range(2):
+                if w < 3:
+                    pt = l1_pool.tile([P, F], F32, name="pt", tag="l1")
+                else:
+                    pt = m_pool.tile([P, F], F32, name="pt", tag="mt%d" % st)
+                layer2(w, st, pt[:], True, True)
+                pps[(w, st)] = pt
 
-        halves = [slice(0, S), slice(S, F)]
-        plh = [None, None]
-        g2h = [None, None]
-        plh[0] = two.tile([P, 4, S], BF16, name="planes")
-        for t in range(4):
-            relu_out(w_c, t, halves[0], plh[0])
-        for st in range(2):
-            nc.scalar.copy(out=mts[:, st, :], in_=mt[st][:])
-        regroup_hidden(w_b)
-        plh[1] = two.tile([P, 4, S], BF16, name="planes")
-        for t in range(4):
-            relu_out(w_c, t, halves[1], plh[1])
-
-        h2c_c = four.tile([P, F], U32, name="h2c", align_bytes=64)
-        h2s_c = four.tile([P, F], U8, name="h2s", align_bytes=64)
-        h2q[w_c] = (h2c_c, h2s_c)
-
-        def regroup_last(h):
-            g2h[h] = two.tile([P, S, 4], BF16, name="g2t", align_bytes=64)
-            regroup(nc.vector.tensor_copy, g2h[h][:], plh[h][:])
-
-        def quantise_last(h):
-            nc.vector.quantize_mx(
-                out=h2c_c[:, halves[h]].bitcast(FP8X4),
-                scales=h2s_c[:, halves[h]],
-                in_=g2h[h][:].rearrange("p n t -> p (n t)"),
+        def add_b3(w):
+            da = dap.tile([P, NI, S], F32, name="da")
+            nc.gpsimd.tensor_tensor(
+                out=da[:],
+                in0=dfin[:],
+                in1=b3all[:, w // 2 - 1, :].unsqueeze(1).to_broadcast([P, NI, S]),
+                op=ADD,
             )
+            das[w] = da
 
-        mbs = [None, None]
-        pqs = [None, None]
+        def finish(w):
+            nst = nstp.tile([P, 2, F], F32, name="nst")
+            for st in range(2):
+                nc.vector.scalar_tensor_tensor(
+                    out=nst[:, st, :],
+                    in0=pps[(w, st)][:],
+                    scalar=bias3[:, st, w - 1 : w],
+                    in1=dt[:, st, :],
+                    op0=ADD,
+                    op1=ADD,
+                )
+            nsts[w] = nst
 
-        def turn_sum(ih):
-            mbs[ih] = m_pool.tile([P, 2, S], F32, name="mb", tag="mt%d" % ih)
+        def turn(src, ih):
+            fin = tp_pool.tile([P, 2, S], F32, name="fin", tag="tp")
             for il in range(2):
                 for st in range(2):
+                    i = 2 * ih + il
                     nc.tensor.transpose(
-                        mbs[ih][:, il, P * st : P * st + P],
-                        mts[:, st, P * (2 * ih + il) : P * (2 * ih + il) + P],
-                        ident[:],
+                        fin[:, il, P * st : P * st + P], src[:, st, P * i : P * i + P], ident[:]
                     )
+            return fin
 
-        def last_two_products(ih):
-            pqs[ih] = pp_pool.tile([P, 2, S], F32, name="pq", tag="pp")
-            for il in range(2):
-                cols = slice(P * (2 * ih + il), P * (2 * ih + il) + P)
-                for w in (w_b, w_c):
-                    mx(pqs[ih][:, il, :], h2q[w][0], h2q[w][1], cols, w3q[w][0], w3q[w][1], w == w_b, w == w_c)
+        def leave(w):
+            al = (w - 1) % 2
+            for ih in range(2):
+                rows = slice(2 * ih, 2 * ih + 2)
+                if al == 0:
+                    osts[ih] = opool.tile([P, 2, 2, S], F32, name="ost")
+                ost = osts[ih]
+                if w in DIRECT:
+                    nc.vector.tensor_tensor(
+                        out=ost[:, :, al, :], in0=pps[(w, ih)][:], in1=das[w][:, rows, :], op=ADD
+                    )
+                else:
+                    fin = turn(nsts[w], ih)
+                    nc.scalar.copy(out=ost[:, :, al, :], in_=fin[:])
+                if w <= 2 or w == A - 1:
+                    nc.sync.dma_start(out=outv[:, rows, w - 1, :], in_=ost[:, :, al, :])
+                elif w == A:
+                    nc.sync.dma_start(out=outv[:, rows, w - 1, :], in_=ost[:, :, al, :])
+                elif al == 1:
+                    nc.sync.dma_start(out=outv[:, rows, w - 2 : w, :], in_=ost[:])
 
-        def minus_mean(dst, src, base, ih):
-            pair = slice(2 * ih, 2 * ih + 2)
-            nc.vector.scalar_tensor_tensor(
-                out=dst[:, pair, :], in0=src[:], scalar=-1.0 / A, in1=base[:, pair, :], op0=MULT, op1=ADD
-            )
-
-        def late_product(w):
-            for st in range(2):
-                feature_major(w, st, m_pool, "mt%d" % st)
-                leave_psum(w, st)
-
-        regroup_last(0)
-        h2q[w_b] = quantise(four, F, g2s[w_b], "h2c", "h2s")
-        quantise_last(0)
-        turn_sum(0)
-        last_two_products(0)
-        minus_mean(dpre, mbs[0], sg, 0)
-        minus_mean(dfin, pqs[0], dpre, 0)
-
-        chunks = (
-            [(i, c) for i in (0, 1) for c in range(3)]
-            + [(i, c) for i in (2, 3) for c in range(3)]
-            + [(i, 3) for i in range(NI)]
+        for n in range(-2, NW + 1):
+            step(n)
+        products(1)
+        products(2)
+        nc.scalar.activation(out=dt[:, 0, :], in_=mt[0][:], func=IDENT, bias=gamt[:, 0, :], scale=-1.0 / A)
+        nc.vector.tensor_scalar(
+            out=dt[:, 1, :], in0=mt[1][:], scalar1=-1.0 / A, scalar2=gamt[:, 1, :], op0=MULT, op1=ADD
         )
-        banks = [(l1_pool, "l1"), (tp_pool, "tp")]
-        for k, (i, c) in enumerate(chunks):
-            ost = opool.tile([P, 4, S], F32, name="ost")
-            for h in range(2):
-                pool, tag = banks[h]
-                fin = pool.tile([P, 2, S], F32, name="fin", tag=tag)
-                for al in range(2):
-                    for st in range(2):
-                        nc.tensor.transpose(
-                            fin[:, al, P * st : P * st + P],
-                            advt[:, 4 * c + 2 * h + al, st, P * i : P * i + P],
-                            ident[:],
-                        )
-                nc.vector.tensor_tensor(
-                    out=ost[:, 2 * h : 2 * h + 2, :],
-                    in0=fin[:],
-                    in1=dfin[:, i, :].unsqueeze(1).to_broadcast([P, 2, S]),
-                    op=ADD,
-                )
-            nc.sync.dma_start(out=outv[:, i, 4 * c : 4 * c + 4, :], in_=ost[:])
-            if k == 0:
-                regroup_last(1)
-            if k == 1:
-                turn_sum(1)
-                quantise_last(1)
-            if k == 2:
-                minus_mean(dpre, mbs[1], sg, 1)
-            if k == 3:
-                last_two_products(1)
-            if k == 4:
-                minus_mean(dfin, pqs[1], dpre, 1)
-            if k in (5, 7, 9):
-                late_product(w_a + (k - 5) // 2)
+        finish(1)
+        for ih in range(2):
+            fin = turn(dt, ih)
+            nc.scalar.copy(out=dfin[:, 2 * ih : 2 * ih + 2, :], in_=fin[:])
+        products(3)
+        finish(2)
+        leave(1)
+        for w in DIRECT[0:2]:
+            add_b3(w)
+        finish(3)
+        leave(2)
+        products(4)
+        for w in range(3, NW):
+            if w in DIRECT:
+                leave(w)
+                k = DIRECT.index(w)
+                if k + 2 < len(DIRECT):
+                    add_b3(DIRECT[k + 2])
+                if w + 2 <= A:
+                    products(w + 2)
+            else:
+                if w + 2 <= A:
+                    products(w + 2)
+                leave(w)
+            if w + 2 <= A and w + 1 in DIRECT and w + 2 not in DIRECT:
+                pass
+            if w in DIRECT and w + 1 <= A:
+                finish(w + 1)

@@ -21,7 +21,7 @@ A = 16
 NI = 4
 F = 512
 S = 256
-R3V = 40
+R3V = 48
 NW = A + 1
 DIRECT = (4, 6, 8, 10, 12, 14, 16)
 RAW_BUFS = 4
@@ -42,9 +42,9 @@ def tile_psicritic_pa_kernel(tc, h1, W2, b2, W3, b3, g1, V2, c2, V3, c3, out):
         xpool = ctx.enter_context(tc.tile_pool(name="xpool", bufs=X_BUFS))
         rawp = ctx.enter_context(tc.tile_pool(name="rawp", bufs=RAW_BUFS))
         two = ctx.enter_context(tc.tile_pool(name="two", bufs=2))
-        opool = ctx.enter_context(tc.tile_pool(name="opool", bufs=5))
+        opool = ctx.enter_context(tc.tile_pool(name="opool", bufs=6))
         nstp = ctx.enter_context(tc.tile_pool(name="nstp", bufs=3))
-        dap = ctx.enter_context(tc.tile_pool(name="dap", bufs=3))
+        dap = ctx.enter_context(tc.tile_pool(name="dap", bufs=4))
         tp_pool = ctx.enter_context(tc.psum_pool(name="tp_pool", bufs=2))
         l1_pool = ctx.enter_context(tc.psum_pool(name="l1_pool", bufs=4))
         m_pool = ctx.enter_context(tc.psum_pool(name="m_pool", bufs=1))
@@ -76,6 +76,13 @@ def tile_psicritic_pa_kernel(tc, h1, W2, b2, W3, b3, g1, V2, c2, V3, c3, out):
             )
             raws[(2, w)] = w2raw
 
+        def load_first_w2():
+            w2raw = rawp.tile([P, 4, F], BF16, name="w2raw")
+            for c in range(2):
+                cols = slice(S * c, S * c + S)
+                nc.sync.dma_start(out=w2raw[:, :, cols], in_=V2.rearrange("(p j) n -> p j n", j=4)[:, :, cols])
+            raws[(2, 0)] = w2raw
+
         def load_w3(w):
             w3raw = rawp.tile([P, 4, S], BF16, name="w3raw")
             nc.sync.dma_start(
@@ -99,18 +106,18 @@ def tile_psicritic_pa_kernel(tc, h1, W2, b2, W3, b3, g1, V2, c2, V3, c3, out):
         nc.vector.memset(b3rows[:], 0.0)
 
         xg = const.tile([P, NI, F], BF16, name="xg")
-        load_w2(0)
         nc.sync.dma_start(out=xg[:], in_=g1.rearrange("(i p) k -> p i k", p=P))
-        load_w2(1)
+        load_first_w2()
         nc.sync.dma_start(out=brow[1:NW, :], in_=b2)
         nc.sync.dma_start(out=brow[0:1, :], in_=c2.rearrange("(o f) -> o f", o=1))
         xs[0] = xpool.tile([P, NI, 2, F], BF16, name="xt")
         load_x_half(0, 0)
+        load_w2(1)
+        load_x_half(0, 1)
         load_w2(2)
+        load_w3(0)
         nc.sync.dma_start(out=b3rows[0:A, :], in_=b3)
         nc.sync.dma_start(out=b3rows[A:NW, :], in_=c3.rearrange("(o s) -> o s", o=1))
-        load_w3(0)
-        load_x_half(0, 1)
         load_w3(1)
         load_w2(3)
         load_x(1)
@@ -175,6 +182,18 @@ def tile_psicritic_pa_kernel(tc, h1, W2, b2, W3, b3, g1, V2, c2, V3, c3, out):
             w2q[w] = (codes[:, 0:F], scales[:, 0:F])
             h1q[w] = (codes[:, F : 2 * F], scales[:, F : 2 * F])
 
+        def quantise_first_apart(w):
+            codes = two.tile([P, 2 * F], U32, name="fc", align_bytes=64)
+            scales = two.tile([P, 2 * F], U8, name="fs", align_bytes=64)
+            for cols in (slice(0, F), slice(F, 2 * F)):
+                nc.vector.quantize_mx(
+                    out=codes[:, cols].bitcast(FP8X4),
+                    scales=scales[:, cols],
+                    in_=firsts[w][:, cols, :].rearrange("p n t -> p (n t)"),
+                )
+            w2q[w] = (codes[:, 0:F], scales[:, 0:F])
+            h1q[w] = (codes[:, F : 2 * F], scales[:, F : 2 * F])
+
         def first_tile(w):
             if w not in firsts:
                 firsts[w] = two.tile([P, 2 * F, 4], BF16, name="first", align_bytes=64)
@@ -187,10 +206,10 @@ def tile_psicritic_pa_kernel(tc, h1, W2, b2, W3, b3, g1, V2, c2, V3, c3, out):
             w3q[w] = quantise(const, S, wg3[w], "w3c%d" % w, "w3s%d" % w)
 
         def regroup_w2(w):
-            nc.vector.tensor_copy(
-                out=first_tile(w)[:, 0:F, :].rearrange("p (t m) j -> p m j t", t=4),
-                in_=raws[(2, w)][:].rearrange("p j (m t) -> p m j t", t=4),
-            )
+            dst = first_tile(w)[:, 0:F, :].rearrange("p (t c i) j -> p c j i t", t=4, i=2)
+            src = raws[(2, w)][:].rearrange("p j (c i t) -> p c j i t", t=4, i=2)
+            for part in (slice(0, 32), slice(32, 64)) if w == 0 else (slice(0, 64),):
+                nc.vector.tensor_copy(out=dst[:, part], in_=src[:, part])
 
         def regroup_w3(w):
             w3g = two.tile([P, S, 4], BF16, name="w3g", align_bytes=64)
@@ -257,27 +276,34 @@ def tile_psicritic_pa_kernel(tc, h1, W2, b2, W3, b3, g1, V2, c2, V3, c3, out):
                 layer2(w, st, mt[st][:], w == 0, w == A)
 
         def step(n):
+            if n == A - 1:
+                quantise_first(A)
             if live(n - 1):
                 regroup_hidden(n - 1)
             if live(n):
+                if n == 0:
+                    quantise_first(1)
+                    regroup_w2(2)
                 relu_out(n)
                 regroup_w3(n)
-            if live(n + 1):
-                if n < 1:
-                    regroup_w2(n + 2)
+            if n == -1:
+                quantise_first_apart(0)
+                regroup_w2(1)
+            elif live(n + 1) and 0 < n < A - 1:
                 quantise_first(n + 1)
             if live(n - 1):
                 quantise_hidden(n - 1)
             if live(n + 2):
                 transpose_x(n + 2)
-            if n == -1:
+            if n == -2:
+                regroup_w2(0)
                 prepare_b2()
             if live(n + 1):
                 layer1(n + 1)
             if live(n - 1):
                 quantise_w3(n - 1)
                 add_to_sum(n - 1)
-            if live(n + 2) and (n < -1 or n > 0):
+            if live(n + 2) and n > 0:
                 regroup_w2(n + 2)
             if n == 2:
                 prepare_b3()
@@ -314,7 +340,8 @@ def tile_psicritic_pa_kernel(tc, h1, W2, b2, W3, b3, g1, V2, c2, V3, c3, out):
 
         def add_b3(w):
             da = dap.tile([P, NI, S], F32, name="da")
-            nc.gpsimd.tensor_tensor(
+            engine = nc.vector if w == DIRECT[0] else nc.gpsimd
+            engine.tensor_tensor(
                 out=da[:],
                 in0=dfin[:],
                 in1=b3all[:, w // 2 - 1, :].unsqueeze(1).to_broadcast([P, NI, S]),
@@ -379,26 +406,25 @@ def tile_psicritic_pa_kernel(tc, h1, W2, b2, W3, b3, g1, V2, c2, V3, c3, out):
             fin = turn(dt, ih)
             nc.scalar.copy(out=dfin[:, 2 * ih : 2 * ih + 2, :], in_=fin[:])
         products(3)
+        products(4)
         finish(2)
         leave(1)
-        for w in DIRECT[0:2]:
+        for w in DIRECT[1:3]:
             add_b3(w)
         finish(3)
+        add_b3(DIRECT[0])
         leave(2)
-        products(4)
         for w in range(3, NW):
             if w in DIRECT:
                 leave(w)
                 k = DIRECT.index(w)
-                if k + 2 < len(DIRECT):
-                    add_b3(DIRECT[k + 2])
+                if k + 3 < len(DIRECT):
+                    add_b3(DIRECT[k + 3])
                 if w + 2 <= A:
                     products(w + 2)
             else:
                 if w + 2 <= A:
                     products(w + 2)
                 leave(w)
-            if w + 2 <= A and w + 1 in DIRECT and w + 2 not in DIRECT:
-                pass
             if w in DIRECT and w + 1 <= A:
                 finish(w + 1)

@@ -21,15 +21,15 @@ A = 16
 NI = 4
 F = 512
 S = 256
-R3V = 48
 NW = A + 1
 DIRECT = (4, 6, 8, 10, 12, 14, 16)
+ADD_BY_VECTOR = (4,)
 RAW_BUFS = 4
 X_BUFS = 3
 
 
 def grouped(dst, src):
-    return dst.rearrange("p (c i) t -> p c t i", i=4), src.rearrange("p t (c i) -> p c t i", i=4)
+    return dst.rearrange("p (c i) t -> p c t i", i=8), src.rearrange("p t (c i) -> p c t i", i=8)
 
 
 def tile_psicritic_pa_kernel(tc, h1, W2, b2, W3, b3, g1, V2, c2, V3, c3, out):
@@ -46,7 +46,8 @@ def tile_psicritic_pa_kernel(tc, h1, W2, b2, W3, b3, g1, V2, c2, V3, c3, out):
         nstp = ctx.enter_context(tc.tile_pool(name="nstp", bufs=3))
         dap = ctx.enter_context(tc.tile_pool(name="dap", bufs=4))
         tp_pool = ctx.enter_context(tc.psum_pool(name="tp_pool", bufs=2))
-        l1_pool = ctx.enter_context(tc.psum_pool(name="l1_pool", bufs=4))
+        l1_pool = ctx.enter_context(tc.psum_pool(name="l1_pool", bufs=3))
+        w3_pool = ctx.enter_context(tc.psum_pool(name="w3_pool", bufs=1))
         m_pool = ctx.enter_context(tc.psum_pool(name="m_pool", bufs=1))
         ctx.enter_context(tc.manual_schedule())
 
@@ -54,6 +55,7 @@ def tile_psicritic_pa_kernel(tc, h1, W2, b2, W3, b3, g1, V2, c2, V3, c3, out):
         xs = {}
         firsts = {}
         wg3 = {}
+        banks = {}
         w2q = {}
         w3q = {}
         h1q = {}
@@ -100,6 +102,10 @@ def tile_psicritic_pa_kernel(tc, h1, W2, b2, W3, b3, g1, V2, c2, V3, c3, out):
 
         ident = const.tile([P, P], F32, name="ident")
         make_identity(nc, ident[:])
+        identb = const.tile([P, P], BF16, name="identb")
+        nc.vector.tensor_copy(out=identb[:], in_=ident[:])
+        statew = const.tile([P, P], BF16, name="statew")
+        nc.vector.tensor_scalar_mul(statew[:], ident[:], -float(A))
         brow = const.tile([P, F], BF16, name="brow")
         nc.vector.memset(brow[:], 0.0)
         b3rows = const.tile([P, S], BF16, name="b3rows")
@@ -211,19 +217,21 @@ def tile_psicritic_pa_kernel(tc, h1, W2, b2, W3, b3, g1, V2, c2, V3, c3, out):
             for part in (slice(0, 32), slice(32, 64)) if w == 0 else (slice(0, 64),):
                 nc.vector.tensor_copy(out=dst[:, part], in_=src[:, part])
 
-        def regroup_w3(w):
+        def carry_w3(w):
+            bank = w3_pool.tile([P, 4, S], BF16, name="bank")
+            for u in range(2):
+                nc.tensor.matmul(
+                    bank[:, 2 * u : 2 * u + 2, :].rearrange("p j s -> p (j s)"),
+                    lhsT=(statew if w == 0 else identb)[:],
+                    rhs=raws[(3, w)][:, 2 * u : 2 * u + 2, :].rearrange("p j s -> p (j s)"),
+                    start=True,
+                    stop=True,
+                )
+            banks[w] = bank
+
+        def take_w3(w):
             w3g = two.tile([P, S, 4], BF16, name="w3g", align_bytes=64)
-            raw = raws[(3, w)]
-            dst, src = grouped(w3g[:, R3V:S, :], raw[:, :, R3V:S])
-            if w == 0:
-                nc.scalar.mul(dst, src, -float(A))
-            else:
-                nc.scalar.copy(out=dst, in_=src)
-            dst, src = grouped(w3g[:, 0:R3V, :], raw[:, :, 0:R3V])
-            if w == 0:
-                nc.vector.tensor_scalar_mul(dst, src, -float(A))
-            else:
-                nc.vector.tensor_copy(out=dst, in_=src)
+            nc.scalar.copy(out=w3g[:], in_=banks[w][:].rearrange("p j s -> p s j"))
             wg3[w] = w3g
 
         def transpose_x(w):
@@ -243,10 +251,10 @@ def tile_psicritic_pa_kernel(tc, h1, W2, b2, W3, b3, g1, V2, c2, V3, c3, out):
                     out=g1w[:, S * ih : S * ih + S, :], in_=tp[:].rearrange("p u b -> p b u")
                 )
 
-        def layer1(w):
+        def layer1(w, ts):
             w2c, w2s = w2q[w]
             h1c, h1s = h1q[w]
-            for t in range(4):
+            for t in ts:
                 l1 = l1_pool.tile([P, F], F32, name="l1", tag="l1")
                 mx(l1[:], w2c, w2s, slice(P * t, P * t + P), h1c, h1s, True, True)
                 l1s[(w, t)] = l1
@@ -254,6 +262,12 @@ def tile_psicritic_pa_kernel(tc, h1, W2, b2, W3, b3, g1, V2, c2, V3, c3, out):
         def relu_out(w):
             pls[w] = two.tile([P, 4, F], BF16, name="planes")
             for t in range(4):
+                if t == 1:
+                    layer1(w, (3,))
+                if t == 1 and w == A:
+                    carry_w3(w)
+                if t == 3 and w < A:
+                    take_w3(w)
                 nc.scalar.activation(
                     out=pls[w][:, t, :],
                     in_=l1s[(w, t)][:],
@@ -284,8 +298,11 @@ def tile_psicritic_pa_kernel(tc, h1, W2, b2, W3, b3, g1, V2, c2, V3, c3, out):
                 if n == 0:
                     quantise_first(1)
                     regroup_w2(2)
+                if n < A:
+                    carry_w3(n)
                 relu_out(n)
-                regroup_w3(n)
+                if n == A:
+                    take_w3(n)
             if n == -1:
                 quantise_first_apart(0)
                 regroup_w2(1)
@@ -299,7 +316,7 @@ def tile_psicritic_pa_kernel(tc, h1, W2, b2, W3, b3, g1, V2, c2, V3, c3, out):
                 regroup_w2(0)
                 prepare_b2()
             if live(n + 1):
-                layer1(n + 1)
+                layer1(n + 1, (0, 1, 2))
             if live(n - 1):
                 quantise_w3(n - 1)
                 add_to_sum(n - 1)
@@ -331,7 +348,9 @@ def tile_psicritic_pa_kernel(tc, h1, W2, b2, W3, b3, g1, V2, c2, V3, c3, out):
                     pps[(w, ih)] = pt
                 return
             for st in range(2):
-                if w < 3:
+                if (w, st) == (2, 1):
+                    pt = w3_pool.tile([P, F], F32, name="pt", tag="bank")
+                elif w < 3:
                     pt = l1_pool.tile([P, F], F32, name="pt", tag="l1")
                 else:
                     pt = m_pool.tile([P, F], F32, name="pt", tag="mt%d" % st)
@@ -340,7 +359,7 @@ def tile_psicritic_pa_kernel(tc, h1, W2, b2, W3, b3, g1, V2, c2, V3, c3, out):
 
         def add_b3(w):
             da = dap.tile([P, NI, S], F32, name="da")
-            engine = nc.vector if w == DIRECT[0] else nc.gpsimd
+            engine = nc.vector if w in ADD_BY_VECTOR else nc.gpsimd
             engine.tensor_tensor(
                 out=da[:],
                 in0=dfin[:],

@@ -66,6 +66,7 @@ def tile_psicritic_pa_kernel(tc, h1, W2, b2, W3, b3, g1, V2, c2, V3, c3, out):
         l1s = {}
         nsts = {}
         das = {}
+        b3turned = []
         osts = {}
 
         def live(w):
@@ -150,7 +151,10 @@ def tile_psicritic_pa_kernel(tc, h1, W2, b2, W3, b3, g1, V2, c2, V3, c3, out):
             tpb3 = tp_pool.tile([P, 2, P], F32, name="tpb3", tag="tp")
             for st in range(2):
                 nc.tensor.transpose(tpb3[:, st, :], b3f[:, st, :], ident[:])
-            nc.scalar.copy(out=bias3[:], in_=tpb3[:, :, 0:NW])
+            b3turned.append(tpb3)
+
+        def take_b3():
+            nc.scalar.copy(out=bias3[:], in_=b3turned[0][:, :, 0:NW])
 
         def prepare_gamma():
             bsum = const.tile([P, 2, 1], F32, name="bsum")
@@ -266,7 +270,7 @@ def tile_psicritic_pa_kernel(tc, h1, W2, b2, W3, b3, g1, V2, c2, V3, c3, out):
                     layer1(w, (3,))
                 if t == 1 and w == A:
                     carry_w3(w)
-                if t == 3 and w < A:
+                if t == 3 and w not in (0, A):
                     take_w3(w)
                 nc.scalar.activation(
                     out=pls[w][:, t, :],
@@ -298,33 +302,44 @@ def tile_psicritic_pa_kernel(tc, h1, W2, b2, W3, b3, g1, V2, c2, V3, c3, out):
                 if n == 0:
                     quantise_first(1)
                     regroup_w2(2)
-                if n < A:
+                if n not in (0, A):
                     carry_w3(n)
                 relu_out(n)
                 if n == A:
                     take_w3(n)
+                if n == 3:
+                    take_b3()
             if n == -1:
                 quantise_first_apart(0)
                 regroup_w2(1)
             elif live(n + 1) and 0 < n < A - 1:
                 quantise_first(n + 1)
             if live(n - 1):
+                if n >= A:
+                    quantise_w3(n - 1)
                 quantise_hidden(n - 1)
             if live(n + 2):
                 transpose_x(n + 2)
+            if n == 0:
+                carry_w3(0)
+                take_w3(0)
             if n == -2:
                 regroup_w2(0)
                 prepare_b2()
             if live(n + 1):
                 layer1(n + 1, (0, 1, 2))
             if live(n - 1):
-                quantise_w3(n - 1)
-                add_to_sum(n - 1)
+                if n < A:
+                    quantise_w3(n - 1)
+                if n == A:
+                    add_to_sum(A - 2)
+                if n != A - 1:
+                    add_to_sum(n - 1)
             if live(n + 2) and n > 0:
                 regroup_w2(n + 2)
             if n == 2:
                 prepare_b3()
-            if n == 3:
+            if n == 4:
                 prepare_gamma()
             if live(n + 2 + RAW_BUFS):
                 load_w2(n + 2 + RAW_BUFS)

@@ -21,6 +21,7 @@ A = 16
 NI = 4
 F = 512
 S = 256
+R3V = 48
 NW = A + 1
 DIRECT = (4, 6, 8, 10, 12, 14, 16)
 ADD_BY_VECTOR = (4,)
@@ -222,21 +223,26 @@ def tile_psicritic_pa_kernel(tc, h1, W2, b2, W3, b3, g1, V2, c2, V3, c3, out):
                 nc.vector.tensor_copy(out=dst[:, part], in_=src[:, part])
 
         def carry_w3(w):
-            bank = w3_pool.tile([P, 4, S], BF16, name="bank")
+            w3g = two.tile([P, S, 4], BF16, name="w3g", align_bytes=64)
+            dst, src = grouped(w3g[:, 0:R3V, :], raws[(3, w)][:, :, 0:R3V])
+            if w == 0:
+                nc.vector.tensor_scalar_mul(dst, src, -float(A))
+            else:
+                nc.vector.tensor_copy(out=dst, in_=src)
+            bank = w3_pool.tile([P, 4, S - R3V], BF16, name="bank")
             for u in range(2):
                 nc.tensor.matmul(
-                    bank[:, 2 * u : 2 * u + 2, :].rearrange("p j s -> p (j s)"),
+                    bank[:, 2 * u : 2 * u + 2, :],
                     lhsT=(statew if w == 0 else identb)[:],
-                    rhs=raws[(3, w)][:, 2 * u : 2 * u + 2, :].rearrange("p j s -> p (j s)"),
+                    rhs=raws[(3, w)][:, 2 * u : 2 * u + 2, R3V:S],
                     start=True,
                     stop=True,
                 )
             banks[w] = bank
+            wg3[w] = w3g
 
         def take_w3(w):
-            w3g = two.tile([P, S, 4], BF16, name="w3g", align_bytes=64)
-            nc.scalar.copy(out=w3g[:], in_=banks[w][:].rearrange("p j s -> p s j"))
-            wg3[w] = w3g
+            nc.scalar.copy(out=wg3[w][:, R3V:S, :], in_=banks[w][:].rearrange("p j s -> p s j"))
 
         def transpose_x(w):
             if w == 0:

@@ -21,10 +21,9 @@ A = 16
 NI = 4
 F = 512
 S = 256
-R3V = 48
+R3V = 32
 NW = A + 1
 DIRECT = (4, 6, 8, 10, 12, 14, 16)
-ADD_BY_VECTOR = (4,)
 RAW_BUFS = 4
 X_BUFS = 3
 
@@ -167,6 +166,7 @@ def tile_psicritic_pa_kernel(tc, h1, W2, b2, W3, b3, g1, V2, c2, V3, c3, out):
 
         dt = const.tile([P, 2, F], F32, name="dt")
         dfin = const.tile([P, NI, S], F32, name="dfin")
+        gate = const.tile([P, S], BF16, name="gate")
         mt = [m_pool.tile([P, F], F32, name="mt%d" % st) for st in range(2)]
 
         def mx(dst, lc, ls, lcols, rc, rs, start, stop):
@@ -380,14 +380,14 @@ def tile_psicritic_pa_kernel(tc, h1, W2, b2, W3, b3, g1, V2, c2, V3, c3, out):
 
         def add_b3(w):
             da = dap.tile([P, NI, S], F32, name="da")
-            engine = nc.vector if w in ADD_BY_VECTOR else nc.gpsimd
+            row = gate[:] if w == DIRECT[1] else b3all[:, w // 2 - 1, :]
+            engine = nc.vector if w == DIRECT[0] else nc.gpsimd
             engine.tensor_tensor(
-                out=da[:],
-                in0=dfin[:],
-                in1=b3all[:, w // 2 - 1, :].unsqueeze(1).to_broadcast([P, NI, S]),
-                op=ADD,
+                out=da[:], in0=dfin[:], in1=row.unsqueeze(1).to_broadcast([P, NI, S]), op=ADD
             )
             das[w] = da
+            if w == DIRECT[0]:
+                nc.vector.tensor_copy(out=gate[:], in_=b3all[:, DIRECT[1] // 2 - 1, :])
 
         def finish(w):
             nst = nstp.tile([P, 2, F], F32, name="nst")
@@ -449,10 +449,9 @@ def tile_psicritic_pa_kernel(tc, h1, W2, b2, W3, b3, g1, V2, c2, V3, c3, out):
         products(4)
         finish(2)
         leave(1)
-        for w in DIRECT[1:3]:
+        for w in DIRECT[0:3]:
             add_b3(w)
         finish(3)
-        add_b3(DIRECT[0])
         leave(2)
         for w in range(3, NW):
             if w in DIRECT:

from contextlib import ExitStack

import concourse.mybir as mybir
from concourse.masks import make_identity

FLOPS = 17 * (2 * 512 * 512 * 512 + 2 * 512 * 512 * 256)

F32 = mybir.dt.float32
BF16 = mybir.dt.bfloat16
U32 = mybir.dt.uint32
U8 = mybir.dt.uint8
FP8X4 = mybir.dt.float8_e4m3fn_x4
ADD = mybir.AluOpType.add
MULT = mybir.AluOpType.mult
AXIS_X = mybir.AxisListType.X
RELU = mybir.ActivationFunctionType.Relu
IDENT = mybir.ActivationFunctionType.Identity

P = 128
A = 16
NI = 4
F = 512
S = 256
R3V = 32
NW = A + 1
DIRECT = (4, 6, 8, 10, 12, 14, 16)
RAW_BUFS = 4
X_BUFS = 3


def grouped(dst, src):
    return dst.rearrange("p (c i) t -> p c t i", i=8), src.rearrange("p t (c i) -> p c t i", i=8)


def tile_psicritic_pa_kernel(tc, h1, W2, b2, W3, b3, g1, V2, c2, V3, c3, out):
    nc = tc.nc
    h1v = h1.rearrange("(i p) a k -> p i a k", p=P)
    outv = out.rearrange("(i p) a s -> p i a s", p=P)

    with ExitStack() as ctx:
        const = ctx.enter_context(tc.tile_pool(name="const", bufs=1))
        xpool = ctx.enter_context(tc.tile_pool(name="xpool", bufs=X_BUFS))
        rawp = ctx.enter_context(tc.tile_pool(name="rawp", bufs=RAW_BUFS))
        two = ctx.enter_context(tc.tile_pool(name="two", bufs=2))
        opool = ctx.enter_context(tc.tile_pool(name="opool", bufs=6))
        nstp = ctx.enter_context(tc.tile_pool(name="nstp", bufs=3))
        dap = ctx.enter_context(tc.tile_pool(name="dap", bufs=4))
        tp_pool = ctx.enter_context(tc.psum_pool(name="tp_pool", bufs=2))
        l1_pool = ctx.enter_context(tc.psum_pool(name="l1_pool", bufs=3))
        w3_pool = ctx.enter_context(tc.psum_pool(name="w3_pool", bufs=1))
        m_pool = ctx.enter_context(tc.psum_pool(name="m_pool", bufs=1))
        ctx.enter_context(tc.manual_schedule())

        raws = {}
        xs = {}
        firsts = {}
        wg3 = {}
        banks = {}
        w2q = {}
        w3q = {}
        h1q = {}
        pls = {}
        g2s = {}
        h2q = {}
        pps = {}
        l1s = {}
        nsts = {}
        das = {}
        b3turned = []
        osts = {}

        def live(w):
            return 0 <= w < NW

        def load_w2(w):
            w2raw = rawp.tile([P, 4, F], BF16, name="w2raw")
            nc.sync.dma_start(
                out=w2raw[:], in_=(V2 if w == 0 else W2[w - 1]).rearrange("(p j) n -> p j n", j=4)
            )
            raws[(2, w)] = w2raw

        def load_first_w2():
            w2raw = rawp.tile([P, 4, F], BF16, name="w2raw")
            for c in range(2):
                cols = slice(S * c, S * c + S)
                nc.sync.dma_start(out=w2raw[:, :, cols], in_=V2.rearrange("(p j) n -> p j n", j=4)[:, :, cols])
            raws[(2, 0)] = w2raw

        def load_w3(w):
            w3raw = rawp.tile([P, 4, S], BF16, name="w3raw")
            nc.sync.dma_start(
                out=w3raw[:], in_=(V3 if w == 0 else W3[w - 1]).rearrange("(p j) s -> p j s", j=4)
            )
            raws[(3, w)] = w3raw

        def load_x(pair):
            xt = xpool.tile([P, NI, 2, F], BF16, name="xt")
            nc.sync.dma_start(out=xt[:], in_=h1v[:, :, 2 * pair : 2 * pair + 2, :])
            xs[pair] = xt

        def load_x_half(pair, al):
            nc.sync.dma_start(out=xs[pair][:, :, al, :], in_=h1v[:, :, 2 * pair + al, :])

        ident = const.tile([P, P], F32, name="ident")
        make_identity(nc, ident[:])
        identb = const.tile([P, P], BF16, name="identb")
        nc.vector.tensor_copy(out=identb[:], in_=ident[:])
        statew = const.tile([P, P], BF16, name="statew")
        nc.vector.tensor_scalar_mul(statew[:], ident[:], -float(A))
        brow = const.tile([P, F], BF16, name="brow")
        nc.vector.memset(brow[:], 0.0)
        b3rows = const.tile([P, S], BF16, name="b3rows")
        nc.vector.memset(b3rows[:], 0.0)

        xg = const.tile([P, NI, F], BF16, name="xg")
        nc.sync.dma_start(out=xg[:], in_=g1.rearrange("(i p) k -> p i k", p=P))
        load_first_w2()
        nc.sync.dma_start(out=brow[1:NW, :], in_=b2)
        nc.sync.dma_start(out=brow[0:1, :], in_=c2.rearrange("(o f) -> o f", o=1))
        xs[0] = xpool.tile([P, NI, 2, F], BF16, name="xt")
        load_x_half(0, 0)
        load_w2(1)
        load_x_half(0, 1)
        load_w2(2)
        load_w3(0)
        nc.sync.dma_start(out=b3rows[0:A, :], in_=b3)
        nc.sync.dma_start(out=b3rows[A:NW, :], in_=c3.rearrange("(o s) -> o s", o=1))
        load_w3(1)
        load_w2(3)
        load_x(1)
        load_w3(2)
        load_w3(3)
        load_x(2)

        bias2 = const.tile([P, 4, NW], F32, name="bias2")
        bias3 = const.tile([P, 2, NW], F32, name="bias3")
        gamt = const.tile([P, 2, 1], F32, name="gamt")
        b3all = const.tile([P, A // 2, S], BF16, name="b3all")

        def prepare_b2():
            browf = const.tile([P, 4, P], F32, name="browf")
            nc.vector.tensor_copy(out=browf[:], in_=brow[:].rearrange("p (m t) -> p t m", t=4))
            tpb = l1_pool.tile([P, 4, P], F32, name="tpb", tag="l1")
            for t in range(4):
                nc.tensor.transpose(tpb[:, t, :], browf[:, t, :], ident[:])
            nc.scalar.copy(out=bias2[:], in_=tpb[:, :, 0:NW])

        def prepare_b3():
            b3f = const.tile([P, 2, P], F32, name="b3f")
            nc.vector.tensor_copy(out=b3f[:], in_=b3rows[:].rearrange("p (t m) -> p t m", t=2))
            tpb3 = tp_pool.tile([P, 2, P], F32, name="tpb3", tag="tp")
            for st in range(2):
                nc.tensor.transpose(tpb3[:, st, :], b3f[:, st, :], ident[:])
            b3turned.append(tpb3)

        def take_b3():
            nc.scalar.copy(out=bias3[:], in_=b3turned[0][:, :, 0:NW])

        def prepare_gamma():
            bsum = const.tile([P, 2, 1], F32, name="bsum")
            for st in range(2):
                nc.vector.tensor_reduce(out=bsum[:, st, :], in_=bias3[:, st, 0:A], axis=AXIS_X, op=ADD)
            nc.vector.scalar_tensor_tensor(
                out=gamt[:], in0=bsum[:], scalar=-1.0 / A, in1=bias3[:, :, A:NW], op0=MULT, op1=ADD
            )

        dt = const.tile([P, 2, F], F32, name="dt")
        dfin = const.tile([P, NI, S], F32, name="dfin")
        gate = const.tile([P, S], BF16, name="gate")
        mt = [m_pool.tile([P, F], F32, name="mt%d" % st) for st in range(2)]

        def mx(dst, lc, ls, lcols, rc, rs, start, stop):
            nc.tensor.matmul_mx(
                out=dst,
                lhsT=lc[:, lcols].bitcast(FP8X4),
                lhsT_scale=ls[:, lcols],
                rhs=rc[:].bitcast(FP8X4),
                rhs_scale=rs[:],
                start=start,
                stop=stop,
            )

        def quantise(pool, width, src, cname, sname):
            codes = pool.tile([P, width], U32, name=cname, align_bytes=64)
            scales = pool.tile([P, width], U8, name=sname, align_bytes=64)
            nc.vector.quantize_mx(
                out=codes[:].bitcast(FP8X4), scales=scales[:], in_=src[:].rearrange("p n t -> p (n t)")
            )
            return codes, scales

        def quantise_first(w):
            codes, scales = quantise(two, 2 * F, firsts[w], "fc", "fs")
            w2q[w] = (codes[:, 0:F], scales[:, 0:F])
            h1q[w] = (codes[:, F : 2 * F], scales[:, F : 2 * F])

        def quantise_first_apart(w):
            codes = two.tile([P, 2 * F], U32, name="fc", align_bytes=64)
            scales = two.tile([P, 2 * F], U8, name="fs", align_bytes=64)
            for cols in (slice(0, F), slice(F, 2 * F)):
                nc.vector.quantize_mx(
                    out=codes[:, cols].bitcast(FP8X4),
                    scales=scales[:, cols],
                    in_=firsts[w][:, cols, :].rearrange("p n t -> p (n t)"),
                )
            w2q[w] = (codes[:, 0:F], scales[:, 0:F])
            h1q[w] = (codes[:, F : 2 * F], scales[:, F : 2 * F])

        def first_tile(w):
            if w not in firsts:
                firsts[w] = two.tile([P, 2 * F, 4], BF16, name="first", align_bytes=64)
            return firsts[w]

        def quantise_hidden(w):
            h2q[w] = quantise(const, F, g2s[w], "h2c%d" % w, "h2s%d" % w)

        def quantise_w3(w):
            w3q[w] = quantise(const, S, wg3[w], "w3c%d" % w, "w3s%d" % w)

        def regroup_w2(w):
            dst = first_tile(w)[:, 0:F, :].rearrange("p (t c i) j -> p c j i t", t=4, i=2)
            src = raws[(2, w)][:].rearrange("p j (c i t) -> p c j i t", t=4, i=2)
            for part in (slice(0, 32), slice(32, 64)) if w == 0 else (slice(0, 64),):
                nc.vector.tensor_copy(out=dst[:, part], in_=src[:, part])

        def carry_w3(w):
            w3g = two.tile([P, S, 4], BF16, name="w3g", align_bytes=64)
            dst, src = grouped(w3g[:, 0:R3V, :], raws[(3, w)][:, :, 0:R3V])
            if w == 0:
                nc.vector.tensor_scalar_mul(dst, src, -float(A))
            else:
                nc.vector.tensor_copy(out=dst, in_=src)
            bank = w3_pool.tile([P, 4, S - R3V], BF16, name="bank")
            for u in range(2):
                nc.tensor.matmul(
                    bank[:, 2 * u : 2 * u + 2, :],
                    lhsT=(statew if w == 0 else identb)[:],
                    rhs=raws[(3, w)][:, 2 * u : 2 * u + 2, R3V:S],
                    start=True,
                    stop=True,
                )
            banks[w] = bank
            wg3[w] = w3g

        def take_w3(w):
            nc.scalar.copy(out=wg3[w][:, R3V:S, :], in_=banks[w][:].rearrange("p j s -> p s j"))

        def transpose_x(w):
            if w == 0:
                xw = xg[:].bitcast(F32)
            else:
                xw = xs[(w - 1) // 2][:].bitcast(F32)[:, :, (w - 1) % 2, :]
            g1w = first_tile(w)[:, F : 2 * F, :].bitcast(F32)
            for ih in range(2):
                tp = tp_pool.tile([P, 2, S], F32, name="tp", tag="tp")
                for il in range(2):
                    for u in range(2):
                        nc.tensor.transpose(
                            tp[:, u, P * il : P * il + P], xw[:, 2 * ih + il, u::2], ident[:]
                        )
                nc.scalar.copy(
                    out=g1w[:, S * ih : S * ih + S, :], in_=tp[:].rearrange("p u b -> p b u")
                )

        def layer1(w, ts):
            w2c, w2s = w2q[w]
            h1c, h1s = h1q[w]
            for t in ts:
                l1 = l1_pool.tile([P, F], F32, name="l1", tag="l1")
                mx(l1[:], w2c, w2s, slice(P * t, P * t + P), h1c, h1s, True, True)
                l1s[(w, t)] = l1

        def relu_out(w):
            pls[w] = two.tile([P, 4, F], BF16, name="planes")
            for t in range(4):
                if t == 1:
                    layer1(w, (3,))
                if t == 1 and w == A:
                    carry_w3(w)
                if t == 3 and w not in (0, A):
                    take_w3(w)
                nc.scalar.activation(
                    out=pls[w][:, t, :],
                    in_=l1s[(w, t)][:],
                    func=RELU,
                    bias=bias2[:, t, w : w + 1],
                    scale=1.0,
                )

        def regroup_hidden(w):
            g2t = two.tile([P, F, 4], BF16, name="g2t", align_bytes=64)
            dst, src = grouped(g2t[:], pls[w][:])
            nc.vector.tensor_copy(out=dst, in_=src)
            g2s[w] = g2t

        def layer2(w, st, dst, start, stop):
            mx(dst, w3q[w][0], w3q[w][1], slice(P * st, P * st + P), h2q[w][0], h2q[w][1], start, stop)

        def add_to_sum(w):
            for st in range(2):
                layer2(w, st, mt[st][:], w == 0, w == A)

        def step(n):
            if n == A - 1:
                quantise_first(A)
            if live(n - 1):
                regroup_hidden(n - 1)
            if live(n):
                if n == 0:
                    quantise_first(1)
                    regroup_w2(2)
                if n not in (0, A):
                    carry_w3(n)
                relu_out(n)
                if n == A:
                    take_w3(n)
                if n == 3:
                    take_b3()
            if n == -1:
                quantise_first_apart(0)
                regroup_w2(1)
            elif live(n + 1) and 0 < n < A - 1:
                quantise_first(n + 1)
            if live(n - 1):
                if n >= A:
                    quantise_w3(n - 1)
                quantise_hidden(n - 1)
            if live(n + 2):
                transpose_x(n + 2)
            if n == 0:
                carry_w3(0)
                take_w3(0)
            if n == -2:
                regroup_w2(0)
                prepare_b2()
            if live(n + 1):
                layer1(n + 1, (0, 1, 2))
            if live(n - 1):
                if n < A:
                    quantise_w3(n - 1)
                if n == A:
                    add_to_sum(A - 2)
                if n != A - 1:
                    add_to_sum(n - 1)
            if live(n + 2) and n > 0:
                regroup_w2(n + 2)
            if n == 2:
                prepare_b3()
            if n == 4:
                prepare_gamma()
            if live(n + 2 + RAW_BUFS):
                load_w2(n + 2 + RAW_BUFS)
            if live(n + RAW_BUFS) and n >= 0:
                load_w3(n + RAW_BUFS)
            if n >= 0 and n % 2 == 0 and n // 2 + X_BUFS < A // 2:
                load_x(n // 2 + X_BUFS)
            if n == A // 2:
                nc.sync.dma_start(
                    out=b3all[:],
                    in_=b3.rearrange("(k two) s -> two k s", two=2)[1, :, :].partition_broadcast(P),
                )

        def products(w):
            if w in DIRECT:
                for ih in range(2):
                    pt = l1_pool.tile([P, 2, S], F32, name="pt", tag="l1")
                    for il in range(2):
                        i = 2 * ih + il
                        mx(pt[:, il, :], h2q[w][0], h2q[w][1], slice(P * i, P * i + P), w3q[w][0], w3q[w][1], True, True)
                    pps[(w, ih)] = pt
                return
            for st in range(2):
                if (w, st) == (2, 1):
                    pt = w3_pool.tile([P, F], F32, name="pt", tag="bank")
                elif w < 3:
                    pt = l1_pool.tile([P, F], F32, name="pt", tag="l1")
                else:
                    pt = m_pool.tile([P, F], F32, name="pt", tag="mt%d" % st)
                layer2(w, st, pt[:], True, True)
                pps[(w, st)] = pt

        def add_b3(w):
            da = dap.tile([P, NI, S], F32, name="da")
            row = gate[:] if w == DIRECT[1] else b3all[:, w // 2 - 1, :]
            engine = nc.vector if w == DIRECT[0] else nc.gpsimd
            engine.tensor_tensor(
                out=da[:], in0=dfin[:], in1=row.unsqueeze(1).to_broadcast([P, NI, S]), op=ADD
            )
            das[w] = da
            if w == DIRECT[0]:
                nc.vector.tensor_copy(out=gate[:], in_=b3all[:, DIRECT[1] // 2 - 1, :])

        def finish(w):
            nst = nstp.tile([P, 2, F], F32, name="nst")
            for st in range(2):
                nc.vector.scalar_tensor_tensor(
                    out=nst[:, st, :],
                    in0=pps[(w, st)][:],
                    scalar=bias3[:, st, w - 1 : w],
                    in1=dt[:, st, :],
                    op0=ADD,
                    op1=ADD,
                )
            nsts[w] = nst

        def turn(src, ih):
            fin = tp_pool.tile([P, 2, S], F32, name="fin", tag="tp")
            for il in range(2):
                for st in range(2):
                    i = 2 * ih + il
                    nc.tensor.transpose(
                        fin[:, il, P * st : P * st + P], src[:, st, P * i : P * i + P], ident[:]
                    )
            return fin

        def leave(w):
            al = (w - 1) % 2
            for ih in range(2):
                rows = slice(2 * ih, 2 * ih + 2)
                if al == 0:
                    osts[ih] = opool.tile([P, 2, 2, S], F32, name="ost")
                ost = osts[ih]
                if w in DIRECT:
                    nc.vector.tensor_tensor(
                        out=ost[:, :, al, :], in0=pps[(w, ih)][:], in1=das[w][:, rows, :], op=ADD
                    )
                else:
                    fin = turn(nsts[w], ih)
                    nc.scalar.copy(out=ost[:, :, al, :], in_=fin[:])
                if w <= 2 or w == A - 1:
                    nc.sync.dma_start(out=outv[:, rows, w - 1, :], in_=ost[:, :, al, :])
                elif w == A:
                    nc.sync.dma_start(out=outv[:, rows, w - 1, :], in_=ost[:, :, al, :])
                elif al == 1:
                    nc.sync.dma_start(out=outv[:, rows, w - 2 : w, :], in_=ost[:])

        for n in range(-2, NW + 1):
            step(n)
        products(1)
        products(2)
        nc.scalar.activation(out=dt[:, 0, :], in_=mt[0][:], func=IDENT, bias=gamt[:, 0, :], scale=-1.0 / A)
        nc.vector.tensor_scalar(
            out=dt[:, 1, :], in0=mt[1][:], scalar1=-1.0 / A, scalar2=gamt[:, 1, :], op0=MULT, op1=ADD
        )
        finish(1)
        for ih in range(2):
            fin = turn(dt, ih)
            nc.scalar.copy(out=dfin[:, 2 * ih : 2 * ih + 2, :], in_=fin[:])
        products(3)
        products(4)
        finish(2)
        leave(1)
        for w in DIRECT[0:3]:
            add_b3(w)
        finish(3)
        leave(2)
        for w in range(3, NW):
            if w in DIRECT:
                leave(w)
                k = DIRECT.index(w)
                if k + 3 < len(DIRECT):
                    add_b3(DIRECT[k + 3])
                if w + 2 <= A:
                    products(w + 2)
            else:
                if w + 2 <= A:
                    products(w + 2)
                leave(w)
            if w in DIRECT and w + 1 <= A:
                finish(w + 1)
